import numpy as np
import ml_dtypes

BF16 = ml_dtypes.bfloat16


def bf(x):
    return np.asarray(x, np.float32).astype(BF16)


def f32(x):
    return np.asarray(x, np.float32)


def f64(x):
    return np.asarray(x).astype(np.float64)


def striped(idx):
    return np.tile(idx.reshape(-1, 16).T, (8, 1))


S, D, H, A, N = 1024, 128, 256, 128, 128


def setup_inputs():
    return {"table": bf(np.random.standard_normal((D, S))), "w1": bf(np.random.standard_normal((D, H)) / np.sqrt(D)), "b1": f32(0.2 * np.random.standard_normal((H, 1))), "w2": bf(1.5 * np.random.standard_normal((H, H)) / np.sqrt(H)), "b2": f32(0.2 * np.random.standard_normal((H, 1))), "w3": bf(2.0 * np.random.standard_normal((H, A)) / np.sqrt(H)), "b3": f32(0.2 * np.random.standard_normal((A, 1))), "offs": striped(np.random.permutation(S)[:N])}


def reference(table, w1, b1, w2, b2, w3, b3, offs):
    idx = offs[:16].T.reshape(-1)
    h1 = np.tanh(f64(w1).T @ f64(table)[:, idx] + f64(b1))
    h2 = np.tanh(f64(w2).T @ h1 + f64(b2))
    z = f64(w3).T @ h2 + f64(b3)
    e = np.exp(z)
    return e / e.sum(axis=0, keepdims=True)

@@ -1,0 +1,87 @@
+import concourse.mybir as mybir
+from concourse.masks import make_identity
+
+BF16, F32, U16 = mybir.dt.bfloat16, mybir.dt.float32, mybir.dt.uint16
+TANH = mybir.ActivationFunctionType.Tanh
+EXP = mybir.ActivationFunctionType.Exp
+
+P = 128
+S = 1024
+N = 128
+H = 256
+A = 128
+HB = H // P
+
+FLOPS = 2 * N * (P * H + H * H + H * A)
+
+
+def tile_ppostructuredinsertionmodel_kernel(tc, table, w1, b1, w2, b2, w3, b3, offs, out):
+    nc = tc.nc
+    with (
+        tc.tile_pool(name="held", bufs=1) as held,
+        tc.psum_pool(name="psum", bufs=1) as psum,
+    ):
+        offsets = held.tile([P, N // 16], U16, name="offsets")
+        nc.sync.dma_start(offsets[:], offs)
+        table_sb = held.tile([P, S], BF16, name="table_sb")
+        nc.sync.dma_start(table_sb[:], table)
+        w1_sb = held.tile([P, H], BF16, name="w1_sb")
+        nc.scalar.dma_start(w1_sb[:], w1)
+        w2_sb = held.tile([P, HB, H], BF16, name="w2_sb")
+        nc.scalar.dma_start(w2_sb[:], w2.rearrange("(k p) n -> p k n", p=P))
+        w3_sb = held.tile([P, HB, A], BF16, name="w3_sb")
+        nc.scalar.dma_start(w3_sb[:], w3.rearrange("(k p) a -> p k a", p=P))
+        b1_sb = held.tile([P, HB], F32, name="b1_sb")
+        b2_sb = held.tile([P, HB], F32, name="b2_sb")
+        with nc.allow_non_contiguous_dma(reason="a bias of 256 floats, one element to a partition"):
+            nc.sync.dma_start(b1_sb[:], b1.rearrange("(c p) o -> p (c o)", p=P))
+            nc.sync.dma_start(b2_sb[:], b2.rearrange("(c p) o -> p (c o)", p=P))
+        b3_row = held.tile([1, A], F32, name="b3_row")
+        nc.scalar.dma_start(b3_row[:], b3.rearrange("a o -> o a"))
+
+        ones_row = held.tile([1, N], F32, name="ones_row")
+        nc.vector.memset(ones_row[:], 1.0)
+        identity = held.tile([P, P], F32, name="identity")
+        make_identity(nc, identity[:])
+
+        h1 = held.tile([P, HB, N], BF16, name="h1")
+        for c in range(HB):
+            acc1 = psum.tile([P, N], F32, name=f"acc1_{c}")
+            nc.tensor.matmul(acc1[:], w1_sb[:, c * P : (c + 1) * P], table_sb[:].indirect(offsets[:]))
+            nc.scalar.activation(h1[:, c, :], acc1[:], TANH, bias=b1_sb[:, c : c + 1])
+
+        zT = psum.tile([N, A], F32, name="zT")
+        nc.tensor.matmul(zT[:], ones_row[:], b3_row[:], start=True, stop=False)
+
+        acc2 = [psum.tile([P, N], F32, name=f"acc2_{c}") for c in range(HB)]
+        for k in range(HB):
+            for c in range(HB):
+                nc.tensor.matmul(
+                    acc2[c][:],
+                    w2_sb[:, k, c * P : (c + 1) * P],
+                    h1[:, k, :],
+                    start=(k == 0),
+                    stop=(k == HB - 1),
+                )
+        h2 = held.tile([P, HB, N], BF16, name="h2")
+        for c in range(HB):
+            nc.scalar.activation(h2[:, c, :], acc2[c][:], TANH, bias=b2_sb[:, c : c + 1])
+
+        for k in range(HB):
+            nc.tensor.matmul(zT[:], h2[:, k, :], w3_sb[:, k, :], start=False, stop=(k == HB - 1))
+
+        neg_max = held.tile([N, 1], F32, name="neg_max")
+        nc.vector.reduce_max(neg_max[:], zT[:], axis=mybir.AxisListType.X, negate=True)
+        expT = held.tile([N, A], F32, name="expT")
+        exp_sum = held.tile([N, 1], F32, name="exp_sum")
+        nc.scalar.activation(expT[:], zT[:], EXP, bias=neg_max[:], accum_out=exp_sum[:])
+        inv_sum = held.tile([N, 1], F32, name="inv_sum")
+        nc.vector.reciprocal(inv_sum[:], exp_sum[:])
+        probT = held.tile([N, A], F32, name="probT")
+        nc.vector.tensor_scalar_mul(probT[:], expT[:], inv_sum[:])
+
+        prob_ps = psum.tile([A, N], F32, name="prob_ps")
+        nc.tensor.transpose(prob_ps[:], probT[:], identity[:])
+        prob = held.tile([A, N], F32, name="prob")
+        nc.vector.tensor_copy(prob[:], prob_ps[:])
+        nc.sync.dma_start(out, prob[:])

@@ -41,6 +41,9 @@ def tile_ppostructuredinsertionmodel_kernel(tc, table, w1, b1, w2, b2, w3, b3, o
 
         ones_row = held.tile([1, N], F32, name="ones_row")
         nc.vector.memset(ones_row[:], 1.0)
+
+        table_warmer = held.tile([1, 1], F32, name="table_warmer")
+        nc.scalar.activation(table_warmer[:], ones_row[:, 0:1], TANH)
         identity = held.tile([P, P], F32, name="identity")
         make_identity(nc, identity[:])
 

@@ -21,23 +21,23 @@ def tile_ppostructuredinsertionmodel_kernel(tc, table, w1, b1, w2, b2, w3, b3, o
         tc.tile_pool(name="held", bufs=1) as held,
         tc.psum_pool(name="psum", bufs=1) as psum,
     ):
-        offsets = held.tile([P, N // 16], U16, name="offsets")
-        nc.sync.dma_start(offsets[:], offs)
         table_sb = held.tile([P, S], BF16, name="table_sb")
         nc.sync.dma_start(table_sb[:], table)
+        offsets = held.tile([P, N // 16], U16, name="offsets")
+        nc.sync.dma_start(offsets[:], offs)
         w1_sb = held.tile([P, H], BF16, name="w1_sb")
         nc.scalar.dma_start(w1_sb[:], w1)
-        w2_sb = held.tile([P, HB, H], BF16, name="w2_sb")
-        nc.scalar.dma_start(w2_sb[:], w2.rearrange("(k p) n -> p k n", p=P))
-        w3_sb = held.tile([P, HB, A], BF16, name="w3_sb")
-        nc.scalar.dma_start(w3_sb[:], w3.rearrange("(k p) a -> p k a", p=P))
         b1_sb = held.tile([P, HB], F32, name="b1_sb")
         b2_sb = held.tile([P, HB], F32, name="b2_sb")
         with nc.allow_non_contiguous_dma(reason="a bias of 256 floats, one element to a partition"):
-            nc.sync.dma_start(b1_sb[:], b1.rearrange("(c p) o -> p (c o)", p=P))
-            nc.sync.dma_start(b2_sb[:], b2.rearrange("(c p) o -> p (c o)", p=P))
+            nc.scalar.dma_start(b1_sb[:], b1.rearrange("(c p) o -> p (c o)", p=P))
+            nc.scalar.dma_start(b2_sb[:], b2.rearrange("(c p) o -> p (c o)", p=P))
         b3_row = held.tile([1, A], F32, name="b3_row")
         nc.scalar.dma_start(b3_row[:], b3.rearrange("a o -> o a"))
+        w2_sb = held.tile([P, HB, H], BF16, name="w2_sb")
+        nc.sync.dma_start(w2_sb[:], w2.rearrange("(k p) n -> p k n", p=P))
+        w3_sb = held.tile([P, HB, A], BF16, name="w3_sb")
+        nc.gpsimd.dma_start(w3_sb[:], w3.rearrange("(k p) a -> p k a", p=P))
 
         ones_row = held.tile([1, N], F32, name="ones_row")
         nc.vector.memset(ones_row[:], 1.0)

@@ -27,13 +27,13 @@ def tile_ppostructuredinsertionmodel_kernel(tc, table, w1, b1, w2, b2, w3, b3, o
         nc.sync.dma_start(offsets[:], offs)
         w1_sb = held.tile([P, H], BF16, name="w1_sb")
         nc.scalar.dma_start(w1_sb[:], w1)
+        b3_row = held.tile([1, A], F32, name="b3_row")
+        nc.scalar.dma_start(b3_row[:], b3.rearrange("a o -> o a"))
         b1_sb = held.tile([P, HB], F32, name="b1_sb")
         b2_sb = held.tile([P, HB], F32, name="b2_sb")
         with nc.allow_non_contiguous_dma(reason="a bias of 256 floats, one element to a partition"):
             nc.scalar.dma_start(b1_sb[:], b1.rearrange("(c p) o -> p (c o)", p=P))
             nc.scalar.dma_start(b2_sb[:], b2.rearrange("(c p) o -> p (c o)", p=P))
-        b3_row = held.tile([1, A], F32, name="b3_row")
-        nc.scalar.dma_start(b3_row[:], b3.rearrange("a o -> o a"))
         w2_sb = held.tile([P, HB, H], BF16, name="w2_sb")
         nc.sync.dma_start(w2_sb[:], w2.rearrange("(k p) n -> p k n", p=P))
         w3_sb = held.tile([P, HB, A], BF16, name="w3_sb")
@@ -47,14 +47,14 @@ def tile_ppostructuredinsertionmodel_kernel(tc, table, w1, b1, w2, b2, w3, b3, o
         identity = held.tile([P, P], F32, name="identity")
         make_identity(nc, identity[:])
 
+        zT = psum.tile([N, A], F32, name="zT")
+        nc.tensor.matmul(zT[:], ones_row[:], b3_row[:], start=True, stop=False)
+
         h1 = held.tile([P, HB, N], BF16, name="h1")
         for c in range(HB):
             acc1 = psum.tile([P, N], F32, name=f"acc1_{c}")
             nc.tensor.matmul(acc1[:], w1_sb[:, c * P : (c + 1) * P], table_sb[:].indirect(offsets[:]))
             nc.scalar.activation(h1[:, c, :], acc1[:], TANH, bias=b1_sb[:, c : c + 1])
-
-        zT = psum.tile([N, A], F32, name="zT")
-        nc.tensor.matmul(zT[:], ones_row[:], b3_row[:], start=True, stop=False)
 
         acc2 = [psum.tile([P, N], F32, name=f"acc2_{c}") for c in range(HB)]
         for k in range(HB):

@@ -11,6 +11,7 @@ N = 128
 H = 256
 A = 128
 HB = H // P
+BANK = 512
 
 FLOPS = 2 * N * (P * H + H * H + H * A)
 
@@ -27,17 +28,27 @@ def tile_ppostructuredinsertionmodel_kernel(tc, table, w1, b1, w2, b2, w3, b3, o
         nc.sync.dma_start(offsets[:], offs)
         w1_sb = held.tile([P, H], BF16, name="w1_sb")
         nc.scalar.dma_start(w1_sb[:], w1)
-        b3_row = held.tile([1, A], F32, name="b3_row")
-        nc.scalar.dma_start(b3_row[:], b3.rearrange("a o -> o a"))
         b1_sb = held.tile([P, HB], F32, name="b1_sb")
         b2_sb = held.tile([P, HB], F32, name="b2_sb")
         with nc.allow_non_contiguous_dma(reason="a bias of 256 floats, one element to a partition"):
             nc.scalar.dma_start(b1_sb[:], b1.rearrange("(c p) o -> p (c o)", p=P))
             nc.scalar.dma_start(b2_sb[:], b2.rearrange("(c p) o -> p (c o)", p=P))
+        b3_row = held.tile([1, A], F32, name="b3_row")
+        nc.scalar.dma_start(b3_row[:], b3.rearrange("a o -> o a"))
         w2_sb = held.tile([P, HB, H], BF16, name="w2_sb")
         nc.sync.dma_start(w2_sb[:], w2.rearrange("(k p) n -> p k n", p=P))
         w3_sb = held.tile([P, HB, A], BF16, name="w3_sb")
         nc.gpsimd.dma_start(w3_sb[:], w3.rearrange("(k p) a -> p k a", p=P))
+
+        zeros = held.tile([P, BANK], BF16, name="zeros")
+        nc.gpsimd.memset(zeros[:], 0.0)
+        unread = psum.tile([P, BANK], F32, name="unread")
+
+        def keep_tensor_engine_busy(matmuls):
+            for i in range(matmuls):
+                nc.tensor.matmul(unread[:], zeros[:, 0:P], zeros[:])
+
+        keep_tensor_engine_busy(4)
 
         ones_row = held.tile([1, N], F32, name="ones_row")
         nc.vector.memset(ones_row[:], 1.0)
@@ -47,14 +58,14 @@ def tile_ppostructuredinsertionmodel_kernel(tc, table, w1, b1, w2, b2, w3, b3, o
         identity = held.tile([P, P], F32, name="identity")
         make_identity(nc, identity[:])
 
-        zT = psum.tile([N, A], F32, name="zT")
-        nc.tensor.matmul(zT[:], ones_row[:], b3_row[:], start=True, stop=False)
-
         h1 = held.tile([P, HB, N], BF16, name="h1")
         for c in range(HB):
             acc1 = psum.tile([P, N], F32, name=f"acc1_{c}")
             nc.tensor.matmul(acc1[:], w1_sb[:, c * P : (c + 1) * P], table_sb[:].indirect(offsets[:]))
             nc.scalar.activation(h1[:, c, :], acc1[:], TANH, bias=b1_sb[:, c : c + 1])
+
+        zT = psum.tile([N, A], F32, name="zT")
+        nc.tensor.matmul(zT[:], ones_row[:], b3_row[:], start=True, stop=False)
 
         acc2 = [psum.tile([P, N], F32, name=f"acc2_{c}") for c in range(HB)]
         for k in range(HB):
@@ -72,6 +83,8 @@ def tile_ppostructuredinsertionmodel_kernel(tc, table, w1, b1, w2, b2, w3, b3, o
 
         for k in range(HB):
             nc.tensor.matmul(zT[:], h2[:, k, :], w3_sb[:, k, :], start=False, stop=(k == HB - 1))
+
+        keep_tensor_engine_busy(2)
 
         neg_max = held.tile([N, 1], F32, name="neg_max")
         nc.vector.reduce_max(neg_max[:], zT[:], axis=mybir.AxisListType.X, negate=True)

@@ -11,7 +11,6 @@ N = 128
 H = 256
 A = 128
 HB = H // P
-BANK = 512
 
 FLOPS = 2 * N * (P * H + H * H + H * A)
 
@@ -22,6 +21,16 @@ def tile_ppostructuredinsertionmodel_kernel(tc, table, w1, b1, w2, b2, w3, b3, o
         tc.tile_pool(name="held", bufs=1) as held,
         tc.psum_pool(name="psum", bufs=1) as psum,
     ):
+        zeros = held.tile([P, P], BF16, name="zeros")
+        nc.gpsimd.memset(zeros[:], 0.0)
+        unread = psum.tile([P, P], F32, name="unread")
+
+        def keep_tensor_engine_busy(matmuls):
+            for i in range(matmuls):
+                nc.tensor.matmul(unread[:], zeros[:], zeros[:])
+
+        keep_tensor_engine_busy(16)
+
         table_sb = held.tile([P, S], BF16, name="table_sb")
         nc.sync.dma_start(table_sb[:], table)
         offsets = held.tile([P, N // 16], U16, name="offsets")
@@ -39,16 +48,6 @@ def tile_ppostructuredinsertionmodel_kernel(tc, table, w1, b1, w2, b2, w3, b3, o
         nc.sync.dma_start(w2_sb[:], w2.rearrange("(k p) n -> p k n", p=P))
         w3_sb = held.tile([P, HB, A], BF16, name="w3_sb")
         nc.gpsimd.dma_start(w3_sb[:], w3.rearrange("(k p) a -> p k a", p=P))
-
-        zeros = held.tile([P, BANK], BF16, name="zeros")
-        nc.gpsimd.memset(zeros[:], 0.0)
-        unread = psum.tile([P, BANK], F32, name="unread")
-
-        def keep_tensor_engine_busy(matmuls):
-            for i in range(matmuls):
-                nc.tensor.matmul(unread[:], zeros[:, 0:P], zeros[:])
-
-        keep_tensor_engine_busy(4)
 
         ones_row = held.tile([1, N], F32, name="ones_row")
         nc.vector.memset(ones_row[:], 1.0)
@@ -84,7 +83,7 @@ def tile_ppostructuredinsertionmodel_kernel(tc, table, w1, b1, w2, b2, w3, b3, o
         for k in range(HB):
             nc.tensor.matmul(zT[:], h2[:, k, :], w3_sb[:, k, :], start=False, stop=(k == HB - 1))
 
-        keep_tensor_engine_busy(2)
+        keep_tensor_engine_busy(8)
 
         neg_max = held.tile([N, 1], F32, name="neg_max")
         nc.vector.reduce_max(neg_max[:], zT[:], axis=mybir.AxisListType.X, negate=True)

@@ -25,11 +25,11 @@ def tile_ppostructuredinsertionmodel_kernel(tc, table, w1, b1, w2, b2, w3, b3, o
         nc.gpsimd.memset(zeros[:], 0.0)
         unread = psum.tile([P, P], F32, name="unread")
 
-        def keep_tensor_engine_busy(matmuls):
+        def keep_tensor_engine_busy(matmuls, moving):
             for i in range(matmuls):
-                nc.tensor.matmul(unread[:], zeros[:], zeros[:])
+                nc.tensor.matmul(unread[:], zeros[:], moving)
 
-        keep_tensor_engine_busy(16)
+        keep_tensor_engine_busy(16, zeros[:])
 
         table_sb = held.tile([P, S], BF16, name="table_sb")
         nc.sync.dma_start(table_sb[:], table)
@@ -83,7 +83,7 @@ def tile_ppostructuredinsertionmodel_kernel(tc, table, w1, b1, w2, b2, w3, b3, o
         for k in range(HB):
             nc.tensor.matmul(zT[:], h2[:, k, :], w3_sb[:, k, :], start=False, stop=(k == HB - 1))
 
-        keep_tensor_engine_busy(8)
+        keep_tensor_engine_busy(8, h2[:, HB - 1, :])
 
         neg_max = held.tile([N, 1], F32, name="neg_max")
         nc.vector.reduce_max(neg_max[:], zT[:], axis=mybir.AxisListType.X, negate=True)

@@ -90,13 +90,17 @@ def tile_ppostructuredinsertionmodel_kernel(tc, table, w1, b1, w2, b2, w3, b3, o
         expT = held.tile([N, A], F32, name="expT")
         exp_sum = held.tile([N, 1], F32, name="exp_sum")
         nc.scalar.activation(expT[:], zT[:], EXP, bias=neg_max[:], accum_out=exp_sum[:])
+
+        numer_ps = psum.tile([A, N], F32, name="numer_ps")
+        nc.tensor.transpose(numer_ps[:], expT[:], identity[:])
         inv_sum = held.tile([N, 1], F32, name="inv_sum")
         nc.vector.reciprocal(inv_sum[:], exp_sum[:])
-        probT = held.tile([N, A], F32, name="probT")
-        nc.vector.tensor_scalar_mul(probT[:], expT[:], inv_sum[:])
 
-        prob_ps = psum.tile([A, N], F32, name="prob_ps")
-        nc.tensor.transpose(prob_ps[:], probT[:], identity[:])
+        inv_sum_rows = psum.tile([A, N], F32, name="inv_sum_rows")
+        nc.tensor.transpose(inv_sum_rows[:], inv_sum[:, 0:1].to_broadcast([N, A]), identity[:])
+
+        numer = held.tile([A, N], F32, name="numer")
+        nc.scalar.copy(numer[:], numer_ps[:])
         prob = held.tile([A, N], F32, name="prob")
-        nc.vector.tensor_copy(prob[:], prob_ps[:])
+        nc.vector.tensor_mul(prob[:], numer[:], inv_sum_rows[:])
         nc.sync.dma_start(out, prob[:])

@@ -40,10 +40,10 @@ def tile_ppostructuredinsertionmodel_kernel(tc, table, w1, b1, w2, b2, w3, b3, o
         b1_sb = held.tile([P, HB], F32, name="b1_sb")
         b2_sb = held.tile([P, HB], F32, name="b2_sb")
         with nc.allow_non_contiguous_dma(reason="a bias of 256 floats, one element to a partition"):
-            nc.scalar.dma_start(b1_sb[:], b1.rearrange("(c p) o -> p (c o)", p=P))
-            nc.scalar.dma_start(b2_sb[:], b2.rearrange("(c p) o -> p (c o)", p=P))
+            nc.sync.dma_start(b1_sb[:], b1.rearrange("(c p) o -> p (c o)", p=P))
+            nc.sync.dma_start(b2_sb[:], b2.rearrange("(c p) o -> p (c o)", p=P))
         b3_row = held.tile([1, A], F32, name="b3_row")
-        nc.scalar.dma_start(b3_row[:], b3.rearrange("a o -> o a"))
+        nc.sync.dma_start(b3_row[:], b3.rearrange("a o -> o a"))
         w2_sb = held.tile([P, HB, H], BF16, name="w2_sb")
         nc.sync.dma_start(w2_sb[:], w2.rearrange("(k p) n -> p k n", p=P))
         w3_sb = held.tile([P, HB, A], BF16, name="w3_sb")

@@ -38,14 +38,15 @@ def tile_ppostructuredinsertionmodel_kernel(tc, table, w1, b1, w2, b2, w3, b3, o
         w1_sb = held.tile([P, H], BF16, name="w1_sb")
         nc.scalar.dma_start(w1_sb[:], w1)
         b1_sb = held.tile([P, HB], F32, name="b1_sb")
-        b2_sb = held.tile([P, HB], F32, name="b2_sb")
         with nc.allow_non_contiguous_dma(reason="a bias of 256 floats, one element to a partition"):
             nc.sync.dma_start(b1_sb[:], b1.rearrange("(c p) o -> p (c o)", p=P))
-            nc.sync.dma_start(b2_sb[:], b2.rearrange("(c p) o -> p (c o)", p=P))
         b3_row = held.tile([1, A], F32, name="b3_row")
         nc.sync.dma_start(b3_row[:], b3.rearrange("a o -> o a"))
         w2_sb = held.tile([P, HB, H], BF16, name="w2_sb")
         nc.sync.dma_start(w2_sb[:], w2.rearrange("(k p) n -> p k n", p=P))
+        b2_sb = held.tile([P, HB], F32, name="b2_sb")
+        with nc.allow_non_contiguous_dma(reason="a bias of 256 floats, one element to a partition"):
+            nc.sync.dma_start(b2_sb[:], b2.rearrange("(c p) o -> p (c o)", p=P))
         w3_sb = held.tile([P, HB, A], BF16, name="w3_sb")
         nc.gpsimd.dma_start(w3_sb[:], w3.rearrange("(k p) a -> p k a", p=P))
 

@@ -40,8 +40,9 @@ def tile_ppostructuredinsertionmodel_kernel(tc, table, w1, b1, w2, b2, w3, b3, o
         b1_sb = held.tile([P, HB], F32, name="b1_sb")
         with nc.allow_non_contiguous_dma(reason="a bias of 256 floats, one element to a partition"):
             nc.sync.dma_start(b1_sb[:], b1.rearrange("(c p) o -> p (c o)", p=P))
-        b3_row = held.tile([1, A], F32, name="b3_row")
-        nc.sync.dma_start(b3_row[:], b3.rearrange("a o -> o a"))
+        b3_rows = held.tile([P, A], F32, name="b3_rows")
+        nc.vector.memset(b3_rows[:], 0.0)
+        nc.sync.dma_start(b3_rows[0:1, :], b3.rearrange("a o -> o a"))
         w2_sb = held.tile([P, HB, H], BF16, name="w2_sb")
         nc.sync.dma_start(w2_sb[:], w2.rearrange("(k p) n -> p k n", p=P))
         b2_sb = held.tile([P, HB], F32, name="b2_sb")
@@ -50,11 +51,11 @@ def tile_ppostructuredinsertionmodel_kernel(tc, table, w1, b1, w2, b2, w3, b3, o
         w3_sb = held.tile([P, HB, A], BF16, name="w3_sb")
         nc.gpsimd.dma_start(w3_sb[:], w3.rearrange("(k p) a -> p k a", p=P))
 
-        ones_row = held.tile([1, N], F32, name="ones_row")
-        nc.vector.memset(ones_row[:], 1.0)
+        ones = held.tile([P, N], F32, name="ones")
+        nc.vector.memset(ones[:], 1.0)
 
         table_warmer = held.tile([1, 1], F32, name="table_warmer")
-        nc.scalar.activation(table_warmer[:], ones_row[:, 0:1], TANH)
+        nc.scalar.activation(table_warmer[:], ones[0:1, 0:1], TANH)
         identity = held.tile([P, P], F32, name="identity")
         make_identity(nc, identity[:])
 
@@ -65,7 +66,7 @@ def tile_ppostructuredinsertionmodel_kernel(tc, table, w1, b1, w2, b2, w3, b3, o
             nc.scalar.activation(h1[:, c, :], acc1[:], TANH, bias=b1_sb[:, c : c + 1])
 
         zT = psum.tile([N, A], F32, name="zT")
-        nc.tensor.matmul(zT[:], ones_row[:], b3_row[:], start=True, stop=False)
+        nc.tensor.matmul(zT[:], ones[:], b3_rows[:], start=True, stop=False)
 
         acc2 = [psum.tile([P, N], F32, name=f"acc2_{c}") for c in range(HB)]
         for k in range(HB):

@@ -21,15 +21,16 @@ def tile_ppostructuredinsertionmodel_kernel(tc, table, w1, b1, w2, b2, w3, b3, o
         tc.tile_pool(name="held", bufs=1) as held,
         tc.psum_pool(name="psum", bufs=1) as psum,
     ):
-        zeros = held.tile([P, P], BF16, name="zeros")
-        nc.gpsimd.memset(zeros[:], 0.0)
+        zero_column = held.tile([P, 1], BF16, name="zero_column")
+        nc.gpsimd.memset(zero_column[:], 0.0)
+        zeros = zero_column[:, 0:1].to_broadcast([P, P])
         unread = psum.tile([P, P], F32, name="unread")
 
         def keep_tensor_engine_busy(matmuls, moving):
             for i in range(matmuls):
-                nc.tensor.matmul(unread[:], zeros[:], moving)
+                nc.tensor.matmul(unread[:], zeros, moving)
 
-        keep_tensor_engine_busy(16, zeros[:])
+        keep_tensor_engine_busy(16, zeros)
 
         table_sb = held.tile([P, S], BF16, name="table_sb")
         nc.sync.dma_start(table_sb[:], table)

@@ -39,46 +39,46 @@ def tile_ppostructuredinsertionmodel_kernel(tc, table, w1, b1, w2, b2, w3, b3, o
         w1_sb = held.tile([P, H], BF16, name="w1_sb")
         nc.scalar.dma_start(w1_sb[:], w1)
         b1_sb = held.tile([P, HB], F32, name="b1_sb")
-        with nc.allow_non_contiguous_dma(reason="a bias of 256 floats, one element to a partition"):
-            nc.sync.dma_start(b1_sb[:], b1.rearrange("(c p) o -> p (c o)", p=P))
+        with nc.allow_non_contiguous_dma(reason="a bias of 256 floats, two to a partition"):
+            nc.sync.dma_start(b1_sb[:], b1.rearrange("(p c) o -> p (c o)", p=P))
+        w2_sb = held.tile([P, HB, H], BF16, name="w2_sb")
+        nc.sync.dma_start(w2_sb[:], w2.rearrange("(p k) n -> p k n", p=P))
+        b2_sb = held.tile([P, HB], F32, name="b2_sb")
+        with nc.allow_non_contiguous_dma(reason="a bias of 256 floats, two to a partition"):
+            nc.sync.dma_start(b2_sb[:], b2.rearrange("(p c) o -> p (c o)", p=P))
         b3_rows = held.tile([P, A], F32, name="b3_rows")
         nc.vector.memset(b3_rows[:], 0.0)
         nc.sync.dma_start(b3_rows[0:1, :], b3.rearrange("a o -> o a"))
-        w2_sb = held.tile([P, HB, H], BF16, name="w2_sb")
-        nc.sync.dma_start(w2_sb[:], w2.rearrange("(k p) n -> p k n", p=P))
-        b2_sb = held.tile([P, HB], F32, name="b2_sb")
-        with nc.allow_non_contiguous_dma(reason="a bias of 256 floats, one element to a partition"):
-            nc.sync.dma_start(b2_sb[:], b2.rearrange("(c p) o -> p (c o)", p=P))
+        identity = held.tile([P, P], F32, name="identity")
+        make_identity(nc, identity[:])
         w3_sb = held.tile([P, HB, A], BF16, name="w3_sb")
-        nc.gpsimd.dma_start(w3_sb[:], w3.rearrange("(k p) a -> p k a", p=P))
+        nc.gpsimd.dma_start(w3_sb[:], w3.rearrange("(p k) a -> p k a", p=P))
 
         ones = held.tile([P, N], F32, name="ones")
         nc.vector.memset(ones[:], 1.0)
 
         table_warmer = held.tile([1, 1], F32, name="table_warmer")
         nc.scalar.activation(table_warmer[:], ones[0:1, 0:1], TANH)
-        identity = held.tile([P, P], F32, name="identity")
-        make_identity(nc, identity[:])
 
         h1 = held.tile([P, HB, N], BF16, name="h1")
         for c in range(HB):
             acc1 = psum.tile([P, N], F32, name=f"acc1_{c}")
-            nc.tensor.matmul(acc1[:], w1_sb[:, c * P : (c + 1) * P], table_sb[:].indirect(offsets[:]))
+            nc.tensor.matmul(acc1[:], w1_sb[:, c::HB], table_sb[:].indirect(offsets[:]))
             nc.scalar.activation(h1[:, c, :], acc1[:], TANH, bias=b1_sb[:, c : c + 1])
-
-        zT = psum.tile([N, A], F32, name="zT")
-        nc.tensor.matmul(zT[:], ones[:], b3_rows[:], start=True, stop=False)
 
         acc2 = [psum.tile([P, N], F32, name=f"acc2_{c}") for c in range(HB)]
         for k in range(HB):
             for c in range(HB):
                 nc.tensor.matmul(
                     acc2[c][:],
-                    w2_sb[:, k, c * P : (c + 1) * P],
+                    w2_sb[:, k, c::HB],
                     h1[:, k, :],
                     start=(k == 0),
                     stop=(k == HB - 1),
                 )
+        zT = psum.tile([N, A], F32, name="zT")
+        nc.tensor.matmul(zT[:], ones[:], b3_rows[:], start=True, stop=False)
+
         h2 = held.tile([P, HB, N], BF16, name="h2")
         for c in range(HB):
             nc.scalar.activation(h2[:, c, :], acc2[c][:], TANH, bias=b2_sb[:, c : c + 1])

import concourse.mybir as mybir
from concourse.masks import make_identity

BF16, F32, U16 = mybir.dt.bfloat16, mybir.dt.float32, mybir.dt.uint16
TANH = mybir.ActivationFunctionType.Tanh
EXP = mybir.ActivationFunctionType.Exp

P = 128
S = 1024
N = 128
H = 256
A = 128
HB = H // P

FLOPS = 2 * N * (P * H + H * H + H * A)


def tile_ppostructuredinsertionmodel_kernel(tc, table, w1, b1, w2, b2, w3, b3, offs, out):
    nc = tc.nc
    with (
        tc.tile_pool(name="held", bufs=1) as held,
        tc.psum_pool(name="psum", bufs=1) as psum,
    ):
        zero_column = held.tile([P, 1], BF16, name="zero_column")
        nc.gpsimd.memset(zero_column[:], 0.0)
        zeros = zero_column[:, 0:1].to_broadcast([P, P])
        unread = psum.tile([P, P], F32, name="unread")

        def keep_tensor_engine_busy(matmuls, moving):
            for i in range(matmuls):
                nc.tensor.matmul(unread[:], zeros, moving)

        keep_tensor_engine_busy(16, zeros)

        table_sb = held.tile([P, S], BF16, name="table_sb")
        nc.sync.dma_start(table_sb[:], table)
        offsets = held.tile([P, N // 16], U16, name="offsets")
        nc.sync.dma_start(offsets[:], offs)
        w1_sb = held.tile([P, H], BF16, name="w1_sb")
        nc.scalar.dma_start(w1_sb[:], w1)
        b1_sb = held.tile([P, HB], F32, name="b1_sb")
        with nc.allow_non_contiguous_dma(reason="a bias of 256 floats, two to a partition"):
            nc.sync.dma_start(b1_sb[:], b1.rearrange("(p c) o -> p (c o)", p=P))
        w2_sb = held.tile([P, HB, H], BF16, name="w2_sb")
        nc.sync.dma_start(w2_sb[:], w2.rearrange("(p k) n -> p k n", p=P))
        b2_sb = held.tile([P, HB], F32, name="b2_sb")
        with nc.allow_non_contiguous_dma(reason="a bias of 256 floats, two to a partition"):
            nc.sync.dma_start(b2_sb[:], b2.rearrange("(p c) o -> p (c o)", p=P))
        b3_rows = held.tile([P, A], F32, name="b3_rows")
        nc.vector.memset(b3_rows[:], 0.0)
        nc.sync.dma_start(b3_rows[0:1, :], b3.rearrange("a o -> o a"))
        identity = held.tile([P, P], F32, name="identity")
        make_identity(nc, identity[:])
        w3_sb = held.tile([P, HB, A], BF16, name="w3_sb")
        nc.gpsimd.dma_start(w3_sb[:], w3.rearrange("(p k) a -> p k a", p=P))

        ones = held.tile([P, N], F32, name="ones")
        nc.vector.memset(ones[:], 1.0)

        table_warmer = held.tile([1, 1], F32, name="table_warmer")
        nc.scalar.activation(table_warmer[:], ones[0:1, 0:1], TANH)

        h1 = held.tile([P, HB, N], BF16, name="h1")
        for c in range(HB):
            acc1 = psum.tile([P, N], F32, name=f"acc1_{c}")
            nc.tensor.matmul(acc1[:], w1_sb[:, c::HB], table_sb[:].indirect(offsets[:]))
            nc.scalar.activation(h1[:, c, :], acc1[:], TANH, bias=b1_sb[:, c : c + 1])

        acc2 = [psum.tile([P, N], F32, name=f"acc2_{c}") for c in range(HB)]
        for k in range(HB):
            for c in range(HB):
                nc.tensor.matmul(
                    acc2[c][:],
                    w2_sb[:, k, c::HB],
                    h1[:, k, :],
                    start=(k == 0),
                    stop=(k == HB - 1),
                )
        zT = psum.tile([N, A], F32, name="zT")
        nc.tensor.matmul(zT[:], ones[:], b3_rows[:], start=True, stop=False)

        h2 = held.tile([P, HB, N], BF16, name="h2")
        for c in range(HB):
            nc.scalar.activation(h2[:, c, :], acc2[c][:], TANH, bias=b2_sb[:, c : c + 1])

        for k in range(HB):
            nc.tensor.matmul(zT[:], h2[:, k, :], w3_sb[:, k, :], start=False, stop=(k == HB - 1))

        keep_tensor_engine_busy(8, h2[:, HB - 1, :])

        neg_max = held.tile([N, 1], F32, name="neg_max")
        nc.vector.reduce_max(neg_max[:], zT[:], axis=mybir.AxisListType.X, negate=True)
        expT = held.tile([N, A], F32, name="expT")
        exp_sum = held.tile([N, 1], F32, name="exp_sum")
        nc.scalar.activation(expT[:], zT[:], EXP, bias=neg_max[:], accum_out=exp_sum[:])

        numer_ps = psum.tile([A, N], F32, name="numer_ps")
        nc.tensor.transpose(numer_ps[:], expT[:], identity[:])
        inv_sum = held.tile([N, 1], F32, name="inv_sum")
        nc.vector.reciprocal(inv_sum[:], exp_sum[:])

        inv_sum_rows = psum.tile([A, N], F32, name="inv_sum_rows")
        nc.tensor.transpose(inv_sum_rows[:], inv_sum[:, 0:1].to_broadcast([N, A]), identity[:])

        numer = held.tile([A, N], F32, name="numer")
        nc.scalar.copy(numer[:], numer_ps[:])
        prob = held.tile([A, N], F32, name="prob")
        nc.vector.tensor_mul(prob[:], numer[:], inv_sum_rows[:])
        nc.sync.dma_start(out, prob[:])
